import numpy as np
import ml_dtypes


def mxq(x, axis, fmt="e4m3"):
    dtype, down = {"e4m3": (ml_dtypes.float8_e4m3fn, 7), "e5m2": (ml_dtypes.float8_e5m2, 14)}[fmt]
    v = np.moveaxis(np.asarray(x, np.float32).astype(ml_dtypes.bfloat16).astype(np.float64), axis, -1)
    blocks = v.reshape(v.shape[:-1] + (-1, 32))
    amax = np.abs(blocks).max(-1, keepdims=True)
    byte = np.maximum(np.where(amax > 0, np.frexp(amax)[1] - 1 + 127, 0) - down, 1)
    scale = np.exp2(byte - 127.0)
    codes = (blocks / scale).astype(np.float32).astype(dtype).astype(np.float64)
    return np.moveaxis((codes * scale).reshape(v.shape), -1, axis)


WIDE = False


def mx_kscale(k):
    if not WIDE:
        return np.ones(k)
    levels = np.array([10, -10, 5, -5, 0])
    a = np.random.permutation(np.resize(levels, k // 512 * 4)).reshape(k // 512, 4)
    idx = np.arange(k)
    return np.exp2(a[idx // 512, idx % 128 // 32])


BF16 = ml_dtypes.bfloat16


def bf(x):
    return np.asarray(x, np.float32).astype(BF16)


def f64(x):
    return np.asarray(x).astype(np.float64)


E2M1 = np.array([0.0, 0.5, 1.0, 1.5, 2.0, 3.0, 4.0, 6.0, -0.0, -0.5, -1.0, -1.5, -2.0, -3.0, -4.0, -6.0])


def pack_weight(w, fmt):
    k, n = w.shape
    w = f64(bf(w)).reshape(k // 32, 32, n)
    amax = np.abs(w).max(1)
    if fmt == "e4m3":
        byte = np.frexp(amax)[1] - 1 + 127 - 7
    else:
        mant, ex = np.frexp(amax / 6.0)
        byte = np.where(mant > 0.5, ex, ex - 1) + 127
    byte = np.clip(np.where(amax > 0, byte, 1), 1, 254)
    scaled = (w * np.exp2(127.0 - byte)[:, None, :]).reshape(k, n).astype(np.float32)
    by_word = np.ascontiguousarray(scaled.reshape(k // 512, 128, 4, n).transpose(0, 1, 3, 2))
    if fmt == "e4m3":
        words = by_word.astype(ml_dtypes.float8_e4m3fn).view(np.uint8)
    else:
        c = by_word.astype(ml_dtypes.float4_e2m1fn).view(np.uint8) & 0xF
        words = c[..., 0::2] | (c[..., 1::2] << 4)
    return np.ascontiguousarray(words), np.ascontiguousarray(byte.astype(np.uint8).reshape(k // 512, 16, n))


def unpack_weight(words, scales, fmt):
    g, p, n, _ = words.shape
    if fmt == "e4m3":
        vals = np.ascontiguousarray(words).view(ml_dtypes.float8_e4m3fn).astype(np.float64)
    else:
        nib = np.empty((g, p, n, 4), np.uint8)
        nib[..., 0::2] = words & 0xF
        nib[..., 1::2] = words >> 4
        vals = E2M1[nib]
    vals = vals * np.repeat(np.exp2(scales.astype(np.float64) - 127.0), 8, axis=1)[..., None]
    return vals.transpose(0, 1, 3, 2).reshape(g * 512, n)

def pack4(w):
    words, scales = pack_weight(w, "e2m1")
    return words.reshape(words.shape[0], 128, -1), scales


def unpack4(words, scales):
    return unpack_weight(words.reshape(words.shape[0], 128, -1, 2), scales, "e2m1")


B, C, H, W, KS, CO = 2, 32, 163, 163, 4, 128
OH, OW = H - KS + 1, W - KS + 1
Q = C * KS * KS


def unfold_patches(x, k):
    oh, ow = x.shape[2] - k + 1, x.shape[3] - k + 1
    rows = []
    for di in range(k):
        cols = [x[:, :, di:di + oh, dj:dj + ow] for dj in range(k)]
        rows.append(np.stack(cols, axis=-1))
    return np.stack(rows, axis=-2)


def wide_factors():
    s = mx_kscale(Q)
    hi, lo = np.log2(s.max()), np.log2(s.min())
    n = np.arange(C)
    phi = np.exp2(np.round(hi + (lo - hi) * np.minimum(n, C - n) / (C / 2)))
    c, h, w = np.ogrid[:C, :H, :W]
    m, di, dj = np.ogrid[:C, :KS, :KS]
    return phi[(c * OH * OW + h * OW + w) % C], phi[(m + di * OW + dj) % C].reshape(Q)


def setup_inputs():
    fx, fw = wide_factors()
    x = bf(np.random.standard_normal((B, C, H, W)) * fx)
    words, scales = pack4(np.random.standard_normal((Q, CO)) / np.sqrt(Q) / fw[:, None])
    bias = bf(np.random.standard_normal(CO) * 0.3)
    return {"x": x, "weights_words": words, "weights_scales": scales, "bias": bias}


def reference(x, weights_words, weights_scales, bias):
    patches = unfold_patches(f64(x), KS)
    patches = patches.reshape(B, OH, OW, Q)
    out = (mxq(patches, 3, "e4m3") @ unpack4(weights_words, weights_scales)) + f64(bias)
    return np.transpose(out, (0, 3, 1, 2))

@@ -1,0 +1,201 @@
+from contextlib import ExitStack
+
+import concourse.mybir as mybir
+from concourse.masks import make_identity
+
+BF16 = mybir.dt.bfloat16
+F32 = mybir.dt.float32
+I32 = mybir.dt.int32
+U32 = mybir.dt.uint32
+U8 = mybir.dt.uint8
+FP8X4 = mybir.dt.float8_e4m3fn_x4
+FP4X4 = mybir.dt.float4_e2m1fn_x4
+
+P = 128
+BATCH, CHANNELS, HEIGHT, WIDTH, KS, C_OUT = 2, 32, 163, 163, 4, 128
+OUT_H = HEIGHT - KS + 1
+OUT_W = WIDTH - KS + 1
+M_SPAN = 32
+J_BLOCKS = OUT_W // M_SPAN
+
+WINDOWS = 20
+ROW_GROUPS = OUT_H // WINDOWS
+CH_GROUP = P // ROW_GROUPS
+GROUPS = BATCH * CHANNELS // CH_GROUP
+ROWS_HELD = WINDOWS + KS - 1
+WORDS = (OUT_W + 2) // 2
+ROW_PITCH = 176
+SHIFTS = WINDOWS * J_BLOCKS
+SHIFTS_PER_PASS = 4
+PASSES = SHIFTS // SHIFTS_PER_PASS
+ALL_PASSES = GROUPS * PASSES
+N_PASS = SHIFTS_PER_PASS * P
+VECTOR_TAKES_EVERY = 3
+STORE_PIECES = 4
+
+FLOPS = 2 * BATCH * OUT_H * OUT_W * (CHANNELS * KS * KS) * C_OUT
+
+
+def tile_conv2d_kernel(tc, x, weights_words, weights_scales, bias, out):
+    nc = tc.nc
+    with ExitStack() as ctx:
+        consts = ctx.enter_context(tc.tile_pool(name="consts", bufs=1))
+        image_pool = ctx.enter_context(tc.tile_pool(name="image", bufs=2))
+        woven_pool = ctx.enter_context(tc.tile_pool(name="woven", bufs=4))
+        patch_pool = ctx.enter_context(tc.tile_pool(name="patch", bufs=3))
+        mx_pool = ctx.enter_context(tc.tile_pool(name="mx", bufs=3))
+        result_pool = ctx.enter_context(tc.tile_pool(name="result", bufs=2))
+        turned_pool = ctx.enter_context(tc.psum_pool(name="turned", bufs=6))
+        acc_pool = ctx.enter_context(tc.psum_pool(name="acc", bufs=2))
+        ctx.enter_context(tc.manual_schedule())
+
+        images = {}
+        wovens = {}
+        turneds = {}
+        patches = {}
+        codes = {}
+        planes = {}
+        accs = {}
+        results = {}
+
+        def load_image_rows(g):
+            image = image_pool.tile([P, 2, ROWS_HELD, ROW_PITCH], BF16, name="image", tag="image")
+            images[g] = image
+            b, c0 = divmod(g * CH_GROUP, CHANNELS)
+            last = (ROW_GROUPS - 1) * WINDOWS + 1
+            for row in range(ROWS_HELD):
+                for s in range(2):
+                    nc.sync.dma_start(
+                        out=image[:, s, row, 0 : 2 * WORDS],
+                        in_=x[b, c0 : c0 + CH_GROUP, row : row + last : WINDOWS, s : s + 2 * WORDS],
+                    )
+
+        def weave(g, a):
+            woven = woven_pool.tile([P, WORDS, 2, KS], F32, name="woven", tag="woven")
+            wovens[(g, a)] = woven
+            words = images[g].bitcast(F32)
+            for s in range(2):
+                nc.vector.tensor_copy(
+                    out=woven[:, :, s, :],
+                    in_=words[:, s, a : a + KS, 0:WORDS].rearrange("n d w -> n w d"),
+                )
+
+        def weave_for(step):
+            if step >= ALL_PASSES:
+                return
+            g, q = divmod(step, PASSES)
+            for shift in range(SHIFTS_PER_PASS * q, SHIFTS_PER_PASS * (q + 1)):
+                if shift % J_BLOCKS == 0:
+                    weave(g, shift // J_BLOCKS)
+
+        def turn(step):
+            g, q = divmod(step, PASSES)
+            for t in range(2):
+                turned = turned_pool.tile([P, N_PASS], F32, name="turned", tag="turned")
+                turneds[(step, t)] = turned
+                for k in range(2):
+                    a, jb = divmod(SHIFTS_PER_PASS * q + 2 * t + k, J_BLOCKS)
+                    flat = wovens[(g, a)].rearrange("n w s d -> n (w s d)")
+                    for u in range(2):
+                        first = 2 * KS * (M_SPAN // 2 * jb + u)
+                        nc.tensor.transpose(
+                            turned[:, (2 * k + u) * P : (2 * k + u + 1) * P],
+                            flat[:, first : first + P],
+                            identity[:],
+                        )
+
+        def gather(step):
+            patch = patch_pool.tile([P, 4 * N_PASS], BF16, name="patch", tag="patch", align_bytes=64)
+            patches[step] = patch
+            words = patch.bitcast(F32)
+            for t in range(2):
+                src = turneds[(step, t)].rearrange("p (k u n) -> p k n u", k=2, u=2)
+                dst = words[:, t * N_PASS : (t + 1) * N_PASS].rearrange("p (k n u) -> p k n u", k=2, u=2)
+                if (2 * step + t) % VECTOR_TAKES_EVERY == 0:
+                    nc.vector.tensor_copy(out=dst, in_=src)
+                else:
+                    nc.scalar.copy(out=dst, in_=src)
+
+        def quantise(step):
+            code = mx_pool.tile([P, N_PASS], U32, name="code", tag="code", align_bytes=64)
+            plane = mx_pool.tile([P, N_PASS], U8, name="plane", tag="plane", align_bytes=64)
+            codes[step] = code
+            planes[step] = plane
+            nc.vector.quantize_mx(out=code[:].bitcast(FP8X4), scales=plane[:], in_=patches[step][:])
+
+        def multiply(step):
+            acc = acc_pool.tile([P, N_PASS], F32, name="acc", tag="acc")
+            accs[step] = acc
+            nc.tensor.matmul_mx(
+                out=acc[:],
+                lhsT=w_words[:].bitcast(FP4X4),
+                lhsT_scale=w_plane[:],
+                rhs=codes[step][:].bitcast(FP8X4),
+                rhs_scale=planes[step][:],
+                start=True,
+                stop=True,
+            )
+
+        def add_bias(step):
+            g, q = divmod(step, PASSES)
+            if q == 0:
+                results[g] = result_pool.tile([P, P, SHIFTS], F32, name="result", tag="result")
+            nc.scalar.activation(
+                out=results[g][:, :, SHIFTS_PER_PASS * q : SHIFTS_PER_PASS * (q + 1)],
+                in_=accs[step].rearrange("o (k n) -> o n k", k=SHIFTS_PER_PASS),
+                func=mybir.ActivationFunctionType.Identity,
+                bias=bias_col[:, 0:1],
+            )
+            if q == PASSES - 1:
+                store(g)
+
+        def store(g):
+            b, c0 = divmod(g * CH_GROUP, CHANNELS)
+            rows_of_a = out[b].rearrange("o u v -> o (u v)")
+            first = c0 * OUT_H * J_BLOCKS
+            sites = P // STORE_PIECES
+            for piece in range(STORE_PIECES):
+                lo = first + piece * sites * SHIFTS
+                nc.sync.dma_start(
+                    out=rows_of_a[:, lo : lo + sites * SHIFTS],
+                    in_=results[g][:, piece * sites : (piece + 1) * sites, :].rearrange("o n k -> o (n k)"),
+                )
+
+        identity = consts.tile([P, P], F32, name="identity")
+        make_identity(nc, identity[:])
+
+        w_words = consts.tile([P, 2 * C_OUT], U8, name="w_words", align_bytes=64)
+        w_plane = consts.tile([P, C_OUT], U8, name="w_plane", align_bytes=64)
+        bias_rows = consts.tile([P, P], BF16, name="bias_rows")
+        bias_wide = consts.tile([P, P], F32, name="bias_wide")
+        bias_col = consts.tile([P, 1], F32, name="bias_col")
+        nc.vector.memset(w_plane[:].bitcast(I32), 0)
+        nc.vector.memset(bias_rows[:], 0.0)
+        nc.sync.dma_start(out=bias_rows[0:1, :], in_=bias.rearrange("(o n) -> o n", o=1))
+        nc.sync.dma_start(out=w_words[:].bitcast(I32), in_=weights_words[0].bitcast(I32))
+        for quadrant in range(4):
+            nc.sync.dma_start(
+                out=w_plane[32 * quadrant : 32 * quadrant + 4, :].bitcast(I32),
+                in_=weights_scales[0, 4 * quadrant : 4 * quadrant + 4, :].bitcast(I32),
+            )
+        load_image_rows(0)
+
+        nc.vector.tensor_copy(out=bias_wide[:], in_=bias_rows[:])
+        bias_turned = turned_pool.tile([P, N_PASS], F32, name="bias_turned", tag="turned")
+        nc.tensor.transpose(bias_turned[:, 0:P], bias_wide[:], identity[:])
+        nc.vector.tensor_copy(out=bias_col[:, 0:1], in_=bias_turned[:, 0:1])
+
+        weave_for(0)
+        for step in range(ALL_PASSES + 3):
+            if step % PASSES == 0 and step // PASSES + 1 < GROUPS:
+                load_image_rows(step // PASSES + 1)
+            weave_for(step + 1)
+            if step < ALL_PASSES:
+                turn(step)
+            if 0 <= step - 1 < ALL_PASSES:
+                gather(step - 1)
+            if 0 <= step - 2 < ALL_PASSES:
+                quantise(step - 2)
+            if 0 <= step - 3 < ALL_PASSES:
+                multiply(step - 3)
+                add_bias(step - 3)

@@ -19,83 +19,88 @@ M_SPAN = 32
 J_BLOCKS = OUT_W // M_SPAN
 
 WINDOWS = 20
-ROW_GROUPS = OUT_H // WINDOWS
-CH_GROUP = P // ROW_GROUPS
+RUNS = OUT_H // WINDOWS
+CH_GROUP = P // RUNS
 GROUPS = BATCH * CHANNELS // CH_GROUP
 ROWS_HELD = WINDOWS + KS - 1
+UNITS_PER_GROUP = WINDOWS // KS
+UNITS = GROUPS * UNITS_PER_GROUP
 WORDS = (OUT_W + 2) // 2
 ROW_PITCH = 176
 SHIFTS = WINDOWS * J_BLOCKS
-SHIFTS_PER_PASS = 4
-PASSES = SHIFTS // SHIFTS_PER_PASS
-ALL_PASSES = GROUPS * PASSES
-N_PASS = SHIFTS_PER_PASS * P
-VECTOR_TAKES_EVERY = 3
+QUAD_COLS = J_BLOCKS * P
+WIDE = 4 * P
+BANKS_PER_UNIT = KS * J_BLOCKS // 4
+LOAD_AHEAD = 4
+TURN_AHEAD = 2
 STORE_PIECES = 4
 
 FLOPS = 2 * BATCH * OUT_H * OUT_W * (CHANNELS * KS * KS) * C_OUT
+
+
+def quads_first_needed_by(unit):
+    if not 0 <= unit < UNITS:
+        return []
+    g, t = divmod(unit, UNITS_PER_GROUP)
+    return [(g, 0), (g, 1)] if t == 0 else [(g, t + 1)]
 
 
 def tile_conv2d_kernel(tc, x, weights_words, weights_scales, bias, out):
     nc = tc.nc
     with ExitStack() as ctx:
         consts = ctx.enter_context(tc.tile_pool(name="consts", bufs=1))
-        image_pool = ctx.enter_context(tc.tile_pool(name="image", bufs=2))
-        woven_pool = ctx.enter_context(tc.tile_pool(name="woven", bufs=4))
-        patch_pool = ctx.enter_context(tc.tile_pool(name="patch", bufs=3))
-        mx_pool = ctx.enter_context(tc.tile_pool(name="mx", bufs=3))
+        image_pool = ctx.enter_context(tc.tile_pool(name="image", bufs=6))
+        woven_pool = ctx.enter_context(tc.tile_pool(name="woven", bufs=3))
+        quad_pool = ctx.enter_context(tc.tile_pool(name="quad", bufs=10))
+        mx_pool = ctx.enter_context(tc.tile_pool(name="mx", bufs=14))
         result_pool = ctx.enter_context(tc.tile_pool(name="result", bufs=2))
-        turned_pool = ctx.enter_context(tc.psum_pool(name="turned", bufs=6))
-        acc_pool = ctx.enter_context(tc.psum_pool(name="acc", bufs=2))
+        turned_pool = ctx.enter_context(tc.psum_pool(name="turned", bufs=4))
+        acc_pool = ctx.enter_context(tc.psum_pool(name="acc", bufs=4))
         ctx.enter_context(tc.manual_schedule())
 
         images = {}
         wovens = {}
         turneds = {}
-        patches = {}
+        quads = {}
         codes = {}
         planes = {}
-        accs = {}
         results = {}
 
-        def load_image_rows(g):
-            image = image_pool.tile([P, 2, ROWS_HELD, ROW_PITCH], BF16, name="image", tag="image")
-            images[g] = image
+        def load_quad(g, t):
+            image = image_pool.tile([P, 2, KS, ROW_PITCH], BF16, name="image", tag="image")
+            images[(g, t)] = image
             b, c0 = divmod(g * CH_GROUP, CHANNELS)
-            last = (ROW_GROUPS - 1) * WINDOWS + 1
-            for row in range(ROWS_HELD):
-                for s in range(2):
-                    nc.sync.dma_start(
-                        out=image[:, s, row, 0 : 2 * WORDS],
-                        in_=x[b, c0 : c0 + CH_GROUP, row : row + last : WINDOWS, s : s + 2 * WORDS],
-                    )
+            span = (RUNS - 1) * WINDOWS + 1
+            for h in range(KS):
+                row = KS * t + h
+                if row < ROWS_HELD:
+                    for parity in range(2):
+                        nc.sync.dma_start(
+                            out=image[:, parity, h, 0 : 2 * WORDS],
+                            in_=x[b, c0 : c0 + CH_GROUP, row : row + span : WINDOWS, parity : parity + 2 * WORDS],
+                        )
+                else:
+                    nc.vector.memset(image[:, :, h, 0 : 2 * WORDS], 0.0)
 
-        def weave(g, a):
+        def weave(g, t):
             woven = woven_pool.tile([P, WORDS, 2, KS], F32, name="woven", tag="woven")
-            wovens[(g, a)] = woven
-            words = images[g].bitcast(F32)
-            for s in range(2):
+            wovens[(g, t)] = woven
+            words = images[(g, t)].bitcast(F32)
+            for parity in range(2):
                 nc.vector.tensor_copy(
-                    out=woven[:, :, s, :],
-                    in_=words[:, s, a : a + KS, 0:WORDS].rearrange("n d w -> n w d"),
+                    out=woven[:, :, parity, :],
+                    in_=words[:, parity, :, 0:WORDS].rearrange("n h w -> n w h"),
                 )
 
-        def weave_for(step):
-            if step >= ALL_PASSES:
-                return
-            g, q = divmod(step, PASSES)
-            for shift in range(SHIFTS_PER_PASS * q, SHIFTS_PER_PASS * (q + 1)):
-                if shift % J_BLOCKS == 0:
-                    weave(g, shift // J_BLOCKS)
+        def jbs_of_bank(bank):
+            return [jb for jb in (2 * bank, 2 * bank + 1) if jb < J_BLOCKS]
 
-        def turn(step):
-            g, q = divmod(step, PASSES)
-            for t in range(2):
-                turned = turned_pool.tile([P, N_PASS], F32, name="turned", tag="turned")
-                turneds[(step, t)] = turned
-                for k in range(2):
-                    a, jb = divmod(SHIFTS_PER_PASS * q + 2 * t + k, J_BLOCKS)
-                    flat = wovens[(g, a)].rearrange("n w s d -> n (w s d)")
+        def turn(g, t):
+            flat = wovens[(g, t)].rearrange("n w s h -> n (w s h)")
+            for bank in range(3):
+                turned = turned_pool.tile([P, WIDE], F32, name="turned", tag="turned")
+                turneds[(g, t, bank)] = turned
+                for k, jb in enumerate(jbs_of_bank(bank)):
                     for u in range(2):
                         first = 2 * KS * (M_SPAN // 2 * jb + u)
                         nc.tensor.transpose(
@@ -104,59 +109,71 @@ def tile_conv2d_kernel(tc, x, weights_words, weights_scales, bias, out):
                             identity[:],
                         )
 
-        def gather(step):
-            patch = patch_pool.tile([P, 4 * N_PASS], BF16, name="patch", tag="patch", align_bytes=64)
-            patches[step] = patch
-            words = patch.bitcast(F32)
-            for t in range(2):
-                src = turneds[(step, t)].rearrange("p (k u n) -> p k n u", k=2, u=2)
-                dst = words[:, t * N_PASS : (t + 1) * N_PASS].rearrange("p (k n u) -> p k n u", k=2, u=2)
-                if (2 * step + t) % VECTOR_TAKES_EVERY == 0:
-                    nc.vector.tensor_copy(out=dst, in_=src)
-                else:
+        def gather(g, t):
+            quad = quad_pool.tile([P, KS * QUAD_COLS], BF16, name="quad", tag="quad", align_bytes=64)
+            quads[(g, t)] = quad
+            words = quad.bitcast(F32)
+            for bank in range(3):
+                n_jb = len(jbs_of_bank(bank))
+                width = n_jb * 2 * P
+                src = turneds[(g, t, bank)][:, 0:width].rearrange("p (k u n) -> p k n u", k=n_jb, u=2)
+                dst = words[:, bank * WIDE : bank * WIDE + width].rearrange("p (k n u) -> p k n u", k=n_jb, u=2)
+                if n_jb == 2:
                     nc.scalar.copy(out=dst, in_=src)
+                else:
+                    nc.vector.tensor_copy(out=dst, in_=src)
 
-        def quantise(step):
-            code = mx_pool.tile([P, N_PASS], U32, name="code", tag="code", align_bytes=64)
-            plane = mx_pool.tile([P, N_PASS], U8, name="plane", tag="plane", align_bytes=64)
-            codes[step] = code
-            planes[step] = plane
-            nc.vector.quantize_mx(out=code[:].bitcast(FP8X4), scales=plane[:], in_=patches[step][:])
+        def quantise(unit, phase):
+            g, t = divmod(unit, UNITS_PER_GROUP)
+            code = mx_pool.tile([P, QUAD_COLS], U32, name="code", tag="code", align_bytes=64)
+            plane = mx_pool.tile([P, QUAD_COLS], U8, name="plane", tag="plane", align_bytes=64)
+            codes[(unit, phase)] = code
+            planes[(unit, phase)] = plane
+            for lo, hi in ((0, WIDE), (WIDE, QUAD_COLS)):
+                nc.vector.quantize_mx(
+                    out=code[:, lo:hi].bitcast(FP8X4),
+                    scales=plane[:, lo:hi],
+                    in_=quads[(g, t)][:, KS * lo : KS * hi],
+                )
 
-        def multiply(step):
-            acc = acc_pool.tile([P, N_PASS], F32, name="acc", tag="acc")
-            accs[step] = acc
-            nc.tensor.matmul_mx(
-                out=acc[:],
-                lhsT=w_words[:].bitcast(FP4X4),
-                lhsT_scale=w_plane[:],
-                rhs=codes[step][:].bitcast(FP8X4),
-                rhs_scale=planes[step][:],
-                start=True,
-                stop=True,
-            )
+        def rotate(unit, phase):
+            g, t = divmod(unit, UNITS_PER_GROUP)
+            nc.sync.dma_start(out=quads[(g, t)][phase:P:KS, :], in_=quads[(g, t + 1)][phase:P:KS, :])
 
-        def add_bias(step):
-            g, q = divmod(step, PASSES)
-            if q == 0:
+        def multiply(unit):
+            g, t = divmod(unit, UNITS_PER_GROUP)
+            if t == 0:
                 results[g] = result_pool.tile([P, P, SHIFTS], F32, name="result", tag="result")
-            nc.scalar.activation(
-                out=results[g][:, :, SHIFTS_PER_PASS * q : SHIFTS_PER_PASS * (q + 1)],
-                in_=accs[step].rearrange("o (k n) -> o n k", k=SHIFTS_PER_PASS),
-                func=mybir.ActivationFunctionType.Identity,
-                bias=bias_col[:, 0:1],
-            )
-            if q == PASSES - 1:
+            for bank in range(BANKS_PER_UNIT):
+                acc = acc_pool.tile([P, WIDE], F32, name="acc", tag="acc")
+                for k in range(4):
+                    phase, jb = divmod(4 * bank + k, J_BLOCKS)
+                    nc.tensor.matmul_mx(
+                        out=acc[:, k * P : (k + 1) * P],
+                        lhsT=w_words[:, (KS - phase) % KS, :].bitcast(FP4X4),
+                        lhsT_scale=w_plane[:],
+                        rhs=codes[(unit, phase)][:, jb * P : (jb + 1) * P].bitcast(FP8X4),
+                        rhs_scale=planes[(unit, phase)][:, jb * P : (jb + 1) * P],
+                        start=True,
+                        stop=True,
+                    )
+                first = KS * J_BLOCKS * t + 4 * bank
+                nc.scalar.activation(
+                    out=results[g][:, :, first : first + 4],
+                    in_=acc.rearrange("o (k n) -> o n k", k=4),
+                    func=mybir.ActivationFunctionType.Identity,
+                    bias=bias_col[:, 0:1],
+                )
+            if t == UNITS_PER_GROUP - 1:
                 store(g)
 
         def store(g):
             b, c0 = divmod(g * CH_GROUP, CHANNELS)
             rows_of_a = out[b].rearrange("o u v -> o (u v)")
-            first = c0 * OUT_H * J_BLOCKS
             sites = P // STORE_PIECES
             for piece in range(STORE_PIECES):
-                lo = first + piece * sites * SHIFTS
-                nc.sync.dma_start(
+                lo = c0 * OUT_H * J_BLOCKS + piece * sites * SHIFTS
+                nc.scalar.dma_start(
                     out=rows_of_a[:, lo : lo + sites * SHIFTS],
                     in_=results[g][:, piece * sites : (piece + 1) * sites, :].rearrange("o n k -> o (n k)"),
                 )
@@ -164,7 +181,7 @@ def tile_conv2d_kernel(tc, x, weights_words, weights_scales, bias, out):
         identity = consts.tile([P, P], F32, name="identity")
         make_identity(nc, identity[:])
 
-        w_words = consts.tile([P, 2 * C_OUT], U8, name="w_words", align_bytes=64)
+        w_words = consts.tile([P, KS, 2 * C_OUT], U8, name="w_words", align_bytes=64)
         w_plane = consts.tile([P, C_OUT], U8, name="w_plane", align_bytes=64)
         bias_rows = consts.tile([P, P], BF16, name="bias_rows")
         bias_wide = consts.tile([P, P], F32, name="bias_wide")
@@ -172,30 +189,39 @@ def tile_conv2d_kernel(tc, x, weights_words, weights_scales, bias, out):
         nc.vector.memset(w_plane[:].bitcast(I32), 0)
         nc.vector.memset(bias_rows[:], 0.0)
         nc.sync.dma_start(out=bias_rows[0:1, :], in_=bias.rearrange("(o n) -> o n", o=1))
-        nc.sync.dma_start(out=w_words[:].bitcast(I32), in_=weights_words[0].bitcast(I32))
+        for g, t in quads_first_needed_by(0):
+            load_quad(g, t)
+
+        w_sbuf = w_words.bitcast(I32)
+        w_dram = weights_words[0].rearrange("(m d) b -> m d b", d=KS).bitcast(I32)
+        for h in range(KS):
+            nc.sync.dma_start(out=w_sbuf[h:P:KS, 0 : KS - h, :], in_=w_dram[:, h:KS, :])
+            if h > 0:
+                nc.sync.dma_start(out=w_sbuf[h:P:KS, KS - h : KS, :], in_=w_dram[:, 0:h, :])
         for quadrant in range(4):
             nc.sync.dma_start(
                 out=w_plane[32 * quadrant : 32 * quadrant + 4, :].bitcast(I32),
                 in_=weights_scales[0, 4 * quadrant : 4 * quadrant + 4, :].bitcast(I32),
             )
-        load_image_rows(0)
 
         nc.vector.tensor_copy(out=bias_wide[:], in_=bias_rows[:])
-        bias_turned = turned_pool.tile([P, N_PASS], F32, name="bias_turned", tag="turned")
+        bias_turned = turned_pool.tile([P, WIDE], F32, name="bias_turned", tag="turned")
         nc.tensor.transpose(bias_turned[:, 0:P], bias_wide[:], identity[:])
         nc.vector.tensor_copy(out=bias_col[:, 0:1], in_=bias_turned[:, 0:1])
 
-        weave_for(0)
-        for step in range(ALL_PASSES + 3):
-            if step % PASSES == 0 and step // PASSES + 1 < GROUPS:
-                load_image_rows(step // PASSES + 1)
-            weave_for(step + 1)
-            if step < ALL_PASSES:
-                turn(step)
-            if 0 <= step - 1 < ALL_PASSES:
-                gather(step - 1)
-            if 0 <= step - 2 < ALL_PASSES:
-                quantise(step - 2)
-            if 0 <= step - 3 < ALL_PASSES:
-                multiply(step - 3)
-                add_bias(step - 3)
+        for step in range(1 - LOAD_AHEAD, UNITS + KS - 1):
+            for g, t in quads_first_needed_by(step + LOAD_AHEAD):
+                load_quad(g, t)
+            for g, t in quads_first_needed_by(step + TURN_AHEAD):
+                weave(g, t)
+                turn(g, t)
+            for phase in reversed(range(KS)):
+                unit = step - phase
+                if 0 <= unit < UNITS:
+                    quantise(unit, phase)
+                    if phase < KS - 1:
+                        rotate(unit, phase)
+            for g, t in quads_first_needed_by(step + TURN_AHEAD):
+                gather(g, t)
+            if 0 <= step - (KS - 1) < UNITS:
+                multiply(step - (KS - 1))

@@ -31,9 +31,10 @@ SHIFTS = WINDOWS * J_BLOCKS
 QUAD_COLS = J_BLOCKS * P
 WIDE = 4 * P
 BANKS_PER_UNIT = KS * J_BLOCKS // 4
-LOAD_AHEAD = 4
+LOAD_AHEAD = 12
 TURN_AHEAD = 2
-STORE_PIECES = 4
+STORE_PIECES = UNITS_PER_GROUP
+PIECE_COLS = P * SHIFTS // STORE_PIECES
 
 FLOPS = 2 * BATCH * OUT_H * OUT_W * (CHANNELS * KS * KS) * C_OUT
 
@@ -49,7 +50,7 @@ def tile_conv2d_kernel(tc, x, weights_words, weights_scales, bias, out):
     nc = tc.nc
     with ExitStack() as ctx:
         consts = ctx.enter_context(tc.tile_pool(name="consts", bufs=1))
-        image_pool = ctx.enter_context(tc.tile_pool(name="image", bufs=6))
+        image_pool = ctx.enter_context(tc.tile_pool(name="image", bufs=16))
         woven_pool = ctx.enter_context(tc.tile_pool(name="woven", bufs=3))
         quad_pool = ctx.enter_context(tc.tile_pool(name="quad", bufs=10))
         mx_pool = ctx.enter_context(tc.tile_pool(name="mx", bufs=14))
@@ -67,30 +68,32 @@ def tile_conv2d_kernel(tc, x, weights_words, weights_scales, bias, out):
         results = {}
 
         def load_quad(g, t):
-            image = image_pool.tile([P, 2, KS, ROW_PITCH], BF16, name="image", tag="image")
+            image = image_pool.tile([P, KS, ROW_PITCH], BF16, name="image", tag="image")
             images[(g, t)] = image
             b, c0 = divmod(g * CH_GROUP, CHANNELS)
             span = (RUNS - 1) * WINDOWS + 1
             for h in range(KS):
                 row = KS * t + h
                 if row < ROWS_HELD:
-                    for parity in range(2):
-                        nc.sync.dma_start(
-                            out=image[:, parity, h, 0 : 2 * WORDS],
-                            in_=x[b, c0 : c0 + CH_GROUP, row : row + span : WINDOWS, parity : parity + 2 * WORDS],
-                        )
+                    nc.sync.dma_start(
+                        out=image[:, h, 0:WIDTH],
+                        in_=x[b, c0 : c0 + CH_GROUP, row : row + span : WINDOWS, :],
+                    )
                 else:
-                    nc.vector.memset(image[:, :, h, 0 : 2 * WORDS], 0.0)
+                    nc.vector.memset(image[:, h, 0:WIDTH], 0.0)
 
         def weave(g, t):
             woven = woven_pool.tile([P, WORDS, 2, KS], F32, name="woven", tag="woven")
             wovens[(g, t)] = woven
-            words = images[(g, t)].bitcast(F32)
-            for parity in range(2):
-                nc.vector.tensor_copy(
-                    out=woven[:, :, parity, :],
-                    in_=words[:, parity, :, 0:WORDS].rearrange("n h w -> n w h"),
-                )
+            image = images[(g, t)]
+            nc.vector.tensor_copy(
+                out=woven[:, :, 0, :],
+                in_=image.bitcast(F32)[:, :, 0:WORDS].rearrange("n h w -> n w h"),
+            )
+            nc.vector.tensor_copy(
+                out=woven.bitcast(BF16).rearrange("n w s (h e) -> n w s h e", e=2)[:, :, 1, :, :],
+                in_=image[:, :, 1 : 1 + 2 * WORDS].rearrange("n h (w e) -> n w h e", e=2),
+            )
 
         def jbs_of_bank(bank):
             return [jb for jb in (2 * bank, 2 * bank + 1) if jb < J_BLOCKS]
@@ -164,19 +167,15 @@ def tile_conv2d_kernel(tc, x, weights_words, weights_scales, bias, out):
                     func=mybir.ActivationFunctionType.Identity,
                     bias=bias_col[:, 0:1],
                 )
-            if t == UNITS_PER_GROUP - 1:
-                store(g)
 
-        def store(g):
+        def store_piece(g, piece):
             b, c0 = divmod(g * CH_GROUP, CHANNELS)
             rows_of_a = out[b].rearrange("o u v -> o (u v)")
-            sites = P // STORE_PIECES
-            for piece in range(STORE_PIECES):
-                lo = c0 * OUT_H * J_BLOCKS + piece * sites * SHIFTS
-                nc.scalar.dma_start(
-                    out=rows_of_a[:, lo : lo + sites * SHIFTS],
-                    in_=results[g][:, piece * sites : (piece + 1) * sites, :].rearrange("o n k -> o (n k)"),
-                )
+            lo = c0 * OUT_H * J_BLOCKS + piece * PIECE_COLS
+            nc.sync.dma_start(
+                out=rows_of_a[:, lo : lo + PIECE_COLS],
+                in_=results[g].rearrange("o n k -> o (n k)")[:, piece * PIECE_COLS : (piece + 1) * PIECE_COLS],
+            )
 
         identity = consts.tile([P, P], F32, name="identity")
         make_identity(nc, identity[:])
@@ -209,18 +208,20 @@ def tile_conv2d_kernel(tc, x, weights_words, weights_scales, bias, out):
         nc.tensor.transpose(bias_turned[:, 0:P], bias_wide[:], identity[:])
         nc.vector.tensor_copy(out=bias_col[:, 0:1], in_=bias_turned[:, 0:1])
 
-        for step in range(1 - LOAD_AHEAD, UNITS + KS - 1):
+        for step in range(1 - LOAD_AHEAD, UNITS + KS - 1 + UNITS_PER_GROUP):
             for g, t in quads_first_needed_by(step + LOAD_AHEAD):
                 load_quad(g, t)
             for g, t in quads_first_needed_by(step + TURN_AHEAD):
                 weave(g, t)
                 turn(g, t)
-            for phase in reversed(range(KS)):
+            for phase in range(KS):
                 unit = step - phase
                 if 0 <= unit < UNITS:
                     quantise(unit, phase)
                     if phase < KS - 1:
                         rotate(unit, phase)
+            if 0 <= step - (KS - 1) - UNITS_PER_GROUP < UNITS:
+                store_piece(*divmod(step - (KS - 1) - UNITS_PER_GROUP, STORE_PIECES))
             for g, t in quads_first_needed_by(step + TURN_AHEAD):
                 gather(g, t)
             if 0 <= step - (KS - 1) < UNITS:

@@ -121,10 +121,7 @@ def tile_conv2d_kernel(tc, x, weights_words, weights_scales, bias, out):
                 width = n_jb * 2 * P
                 src = turneds[(g, t, bank)][:, 0:width].rearrange("p (k u n) -> p k n u", k=n_jb, u=2)
                 dst = words[:, bank * WIDE : bank * WIDE + width].rearrange("p (k n u) -> p k n u", k=n_jb, u=2)
-                if n_jb == 2:
-                    nc.scalar.copy(out=dst, in_=src)
-                else:
-                    nc.vector.tensor_copy(out=dst, in_=src)
+                nc.scalar.copy(out=dst, in_=src)
 
         def quantise(unit, phase):
             g, t = divmod(unit, UNITS_PER_GROUP)

@@ -121,7 +121,10 @@ def tile_conv2d_kernel(tc, x, weights_words, weights_scales, bias, out):
                 width = n_jb * 2 * P
                 src = turneds[(g, t, bank)][:, 0:width].rearrange("p (k u n) -> p k n u", k=n_jb, u=2)
                 dst = words[:, bank * WIDE : bank * WIDE + width].rearrange("p (k n u) -> p k n u", k=n_jb, u=2)
-                nc.scalar.copy(out=dst, in_=src)
+                if n_jb == 2 or t % 2 == 1:
+                    nc.scalar.copy(out=dst, in_=src)
+                else:
+                    nc.vector.tensor_copy(out=dst, in_=src)
 
         def quantise(unit, phase):
             g, t = divmod(unit, UNITS_PER_GROUP)

@@ -39,6 +39,35 @@ PIECE_COLS = P * SHIFTS // STORE_PIECES
 FLOPS = 2 * BATCH * OUT_H * OUT_W * (CHANNELS * KS * KS) * C_OUT
 
 
+EARLY_UNITS = 2
+
+
+def banks_due(step):
+    due = []
+    for unit in range(UNITS):
+        for bank in range(BANKS_PER_UNIT):
+            if step == unit + ((4 * bank + 3) // J_BLOCKS if unit >= UNITS - EARLY_UNITS else KS - 1):
+                due.append((unit, bank))
+    return due
+
+
+def passes_of_bank(bank):
+    runs = []
+    for k in range(4):
+        phase, jb = divmod(4 * bank + k, J_BLOCKS)
+        if runs and runs[-1][1] == phase:
+            runs[-1] = (runs[-1][0], phase, runs[-1][2], runs[-1][3] + 1)
+        else:
+            runs.append((k, phase, jb, 1))
+    passes = []
+    for k, phase, jb, n in runs:
+        if n == 3:
+            passes.extend([(k, phase, jb, 2), (k + 2, phase, jb + 2, 1)])
+        else:
+            passes.append((k, phase, jb, n))
+    return passes
+
+
 def quads_first_needed_by(unit):
     if not 0 <= unit < UNITS:
         return []
@@ -143,24 +172,31 @@ def tile_conv2d_kernel(tc, x, weights_words, weights_scales, bias, out):
             g, t = divmod(unit, UNITS_PER_GROUP)
             nc.sync.dma_start(out=quads[(g, t)][phase:P:KS, :], in_=quads[(g, t + 1)][phase:P:KS, :])
 
-        def multiply(unit):
+        def multiply_bank(unit, bank, by_vector):
             g, t = divmod(unit, UNITS_PER_GROUP)
-            if t == 0:
+            if t == 0 and bank == 0:
                 results[g] = result_pool.tile([P, P, SHIFTS], F32, name="result", tag="result")
-            for bank in range(BANKS_PER_UNIT):
-                acc = acc_pool.tile([P, WIDE], F32, name="acc", tag="acc")
-                for k in range(4):
-                    phase, jb = divmod(4 * bank + k, J_BLOCKS)
-                    nc.tensor.matmul_mx(
-                        out=acc[:, k * P : (k + 1) * P],
-                        lhsT=w_words[:, (KS - phase) % KS, :].bitcast(FP4X4),
-                        lhsT_scale=w_plane[:],
-                        rhs=codes[(unit, phase)][:, jb * P : (jb + 1) * P].bitcast(FP8X4),
-                        rhs_scale=planes[(unit, phase)][:, jb * P : (jb + 1) * P],
-                        start=True,
-                        stop=True,
-                    )
-                first = KS * J_BLOCKS * t + 4 * bank
+            acc = acc_pool.tile([P, WIDE], F32, name="acc", tag="acc")
+            for k, phase, jb, n in passes_of_bank(bank):
+                nc.tensor.matmul_mx(
+                    out=acc[:, k * P : (k + n) * P],
+                    lhsT=w_words[:, (KS - phase) % KS, :].bitcast(FP4X4),
+                    lhsT_scale=w_plane[:],
+                    rhs=codes[(unit, phase)][:, jb * P : (jb + n) * P].bitcast(FP8X4),
+                    rhs_scale=planes[(unit, phase)][:, jb * P : (jb + n) * P],
+                    start=True,
+                    stop=True,
+                )
+            first = KS * J_BLOCKS * t + 4 * bank
+            if by_vector:
+                nc.vector.tensor_scalar(
+                    out=results[g][:, :, first : first + 4],
+                    in0=acc.rearrange("o (k n) -> o n k", k=4),
+                    scalar1=bias_col[:, 0:1],
+                    scalar2=None,
+                    op0=mybir.AluOpType.add,
+                )
+            else:
                 nc.scalar.activation(
                     out=results[g][:, :, first : first + 4],
                     in_=acc.rearrange("o (k n) -> o n k", k=4),
@@ -224,5 +260,5 @@ def tile_conv2d_kernel(tc, x, weights_words, weights_scales, bias, out):
                 store_piece(*divmod(step - (KS - 1) - UNITS_PER_GROUP, STORE_PIECES))
             for g, t in quads_first_needed_by(step + TURN_AHEAD):
                 gather(g, t)
-            if 0 <= step - (KS - 1) < UNITS:
-                multiply(step - (KS - 1))
+            for i, (unit, bank) in enumerate(banks_due(step)):
+                multiply_bank(unit, bank, step > UNITS and i % 2 == 1)

@@ -31,7 +31,8 @@ SHIFTS = WINDOWS * J_BLOCKS
 QUAD_COLS = J_BLOCKS * P
 WIDE = 4 * P
 BANKS_PER_UNIT = KS * J_BLOCKS // 4
-LOAD_AHEAD = 12
+FIRST_LOADS = 5
+LOADS_PER_STEP = 3
 TURN_AHEAD = 2
 STORE_PIECES = UNITS_PER_GROUP
 PIECE_COLS = P * SHIFTS // STORE_PIECES
@@ -244,9 +245,11 @@ def tile_conv2d_kernel(tc, x, weights_words, weights_scales, bias, out):
         nc.tensor.transpose(bias_turned[:, 0:P], bias_wide[:], identity[:])
         nc.vector.tensor_copy(out=bias_col[:, 0:1], in_=bias_turned[:, 0:1])
 
-        for step in range(1 - LOAD_AHEAD, UNITS + KS - 1 + UNITS_PER_GROUP):
-            for g, t in quads_first_needed_by(step + LOAD_AHEAD):
-                load_quad(g, t)
+        load_order = [quad for unit in range(UNITS) for quad in quads_first_needed_by(unit)]
+        for g, t in load_order[len(quads_first_needed_by(0)) : FIRST_LOADS]:
+            load_quad(g, t)
+
+        for step in range(-TURN_AHEAD, UNITS + KS - 1 + UNITS_PER_GROUP):
             for g, t in quads_first_needed_by(step + TURN_AHEAD):
                 weave(g, t)
                 turn(g, t)
@@ -256,6 +259,9 @@ def tile_conv2d_kernel(tc, x, weights_words, weights_scales, bias, out):
                     quantise(unit, phase)
                     if phase < KS - 1:
                         rotate(unit, phase)
+            if step >= 0:
+                for g, t in load_order[FIRST_LOADS + LOADS_PER_STEP * step : FIRST_LOADS + LOADS_PER_STEP * (step + 1)]:
+                    load_quad(g, t)
             if 0 <= step - (KS - 1) - UNITS_PER_GROUP < UNITS:
                 store_piece(*divmod(step - (KS - 1) - UNITS_PER_GROUP, STORE_PIECES))
             for g, t in quads_first_needed_by(step + TURN_AHEAD):

@@ -26,7 +26,7 @@ ROWS_HELD = WINDOWS + KS - 1
 UNITS_PER_GROUP = WINDOWS // KS
 UNITS = GROUPS * UNITS_PER_GROUP
 WORDS = (OUT_W + 2) // 2
-ROW_PITCH = 176
+PAIR_PITCH = 336
 SHIFTS = WINDOWS * J_BLOCKS
 QUAD_COLS = J_BLOCKS * P
 WIDE = 4 * P
@@ -98,31 +98,32 @@ def tile_conv2d_kernel(tc, x, weights_words, weights_scales, bias, out):
         results = {}
 
         def load_quad(g, t):
-            image = image_pool.tile([P, KS, ROW_PITCH], BF16, name="image", tag="image")
+            image = image_pool.tile([P, KS // 2, PAIR_PITCH], BF16, name="image", tag="image")
             images[(g, t)] = image
             b, c0 = divmod(g * CH_GROUP, CHANNELS)
-            span = (RUNS - 1) * WINDOWS + 1
-            for h in range(KS):
-                row = KS * t + h
-                if row < ROWS_HELD:
-                    nc.sync.dma_start(
-                        out=image[:, h, 0:WIDTH],
-                        in_=x[b, c0 : c0 + CH_GROUP, row : row + span : WINDOWS, :],
-                    )
-                else:
-                    nc.vector.memset(image[:, h, 0:WIDTH], 0.0)
+            skip = KS - 1 if t == UNITS_PER_GROUP else 0
+            runs = x[b, c0 : c0 + CH_GROUP, skip : skip + OUT_H, :].rearrange("c (r k) w -> c r (k w)", k=WINDOWS)
+            if t == UNITS_PER_GROUP:
+                nc.vector.memset(image[:, 1, WIDTH - 1 : 2 * WIDTH], 0.0)
+            for a in range(KS // 2):
+                row = KS * t + 2 * a
+                n_rows = min(2, ROWS_HELD - row)
+                nc.sync.dma_start(
+                    out=image[:, a, 0 : n_rows * WIDTH],
+                    in_=runs[:, :, (row - skip) * WIDTH : (row - skip + n_rows) * WIDTH],
+                )
 
         def weave(g, t):
             woven = woven_pool.tile([P, WORDS, 2, KS], F32, name="woven", tag="woven")
             wovens[(g, t)] = woven
             image = images[(g, t)]
             nc.vector.tensor_copy(
-                out=woven[:, :, 0, :],
-                in_=image.bitcast(F32)[:, :, 0:WORDS].rearrange("n h w -> n w h"),
+                out=woven.rearrange("n w s (a b) -> n w s a b", b=2)[:, :, 0, :, :],
+                in_=image.bitcast(F32)[:, :, 0 : WIDTH + 1].rearrange("n a (b w) -> n w a b", b=2)[:, 0:WORDS, :, :],
             )
             nc.vector.tensor_copy(
-                out=woven.bitcast(BF16).rearrange("n w s (h e) -> n w s h e", e=2)[:, :, 1, :, :],
-                in_=image[:, :, 1 : 1 + 2 * WORDS].rearrange("n h (w e) -> n w h e", e=2),
+                out=woven.bitcast(BF16).rearrange("n w s (a b e) -> n w s a b e", b=2, e=2)[:, :, 1, :, :, :],
+                in_=image[:, :, 1 : 1 + 4 * WORDS].rearrange("n a (b w e) -> n w a b e", b=2, e=2),
             )
 
         def jbs_of_bank(bank):
@@ -229,11 +230,14 @@ def tile_conv2d_kernel(tc, x, weights_words, weights_scales, bias, out):
             load_quad(g, t)
 
         w_sbuf = w_words.bitcast(I32)
-        w_dram = weights_words[0].rearrange("(m d) b -> m d b", d=KS).bitcast(I32)
-        for h in range(KS):
-            nc.sync.dma_start(out=w_sbuf[h:P:KS, 0 : KS - h, :], in_=w_dram[:, h:KS, :])
-            if h > 0:
-                nc.sync.dma_start(out=w_sbuf[h:P:KS, KS - h : KS, :], in_=w_dram[:, 0:h, :])
+        w_dram = weights_words[0].rearrange("(i q) b -> i q b", q=2 * KS).bitcast(I32)
+        for lane in range(2):
+            for h in range(KS):
+                first = KS * ((lane + h) % 2)
+                w_rows = w_sbuf[KS * lane + h : P : 2 * KS, :, :]
+                nc.sync.dma_start(out=w_rows[:, 0 : KS - h, :], in_=w_dram[:, first + h : first + KS, :])
+                if h > 0:
+                    nc.sync.dma_start(out=w_rows[:, KS - h : KS, :], in_=w_dram[:, first : first + h, :])
         for quadrant in range(4):
             nc.sync.dma_start(
                 out=w_plane[32 * quadrant : 32 * quadrant + 4, :].bitcast(I32),

@@ -225,10 +225,14 @@ def tile_conv2d_kernel(tc, x, weights_words, weights_scales, bias, out):
         bias_col = consts.tile([P, 1], F32, name="bias_col")
         nc.vector.memset(w_plane[:].bitcast(I32), 0)
         nc.vector.memset(bias_rows[:], 0.0)
-        nc.sync.dma_start(out=bias_rows[0:1, :], in_=bias.rearrange("(o n) -> o n", o=1))
         for g, t in quads_first_needed_by(0):
             load_quad(g, t)
 
+        load_order = [quad for unit in range(UNITS) for quad in quads_first_needed_by(unit)]
+        for g, t in load_order[len(quads_first_needed_by(0)) : FIRST_LOADS]:
+            load_quad(g, t)
+
+        nc.sync.dma_start(out=bias_rows[0:1, :], in_=bias.rearrange("(o n) -> o n", o=1))
         w_sbuf = w_words.bitcast(I32)
         w_dram = weights_words[0].rearrange("(i q) b -> i q b", q=2 * KS).bitcast(I32)
         for lane in range(2):
@@ -243,15 +247,6 @@ def tile_conv2d_kernel(tc, x, weights_words, weights_scales, bias, out):
                 out=w_plane[32 * quadrant : 32 * quadrant + 4, :].bitcast(I32),
                 in_=weights_scales[0, 4 * quadrant : 4 * quadrant + 4, :].bitcast(I32),
             )
-
-        nc.vector.tensor_copy(out=bias_wide[:], in_=bias_rows[:])
-        bias_turned = turned_pool.tile([P, WIDE], F32, name="bias_turned", tag="turned")
-        nc.tensor.transpose(bias_turned[:, 0:P], bias_wide[:], identity[:])
-        nc.vector.tensor_copy(out=bias_col[:, 0:1], in_=bias_turned[:, 0:1])
-
-        load_order = [quad for unit in range(UNITS) for quad in quads_first_needed_by(unit)]
-        for g, t in load_order[len(quads_first_needed_by(0)) : FIRST_LOADS]:
-            load_quad(g, t)
 
         for step in range(-TURN_AHEAD, UNITS + KS - 1 + UNITS_PER_GROUP):
             for g, t in quads_first_needed_by(step + TURN_AHEAD):
@@ -270,5 +265,10 @@ def tile_conv2d_kernel(tc, x, weights_words, weights_scales, bias, out):
                 store_piece(*divmod(step - (KS - 1) - UNITS_PER_GROUP, STORE_PIECES))
             for g, t in quads_first_needed_by(step + TURN_AHEAD):
                 gather(g, t)
+            if step == 0:
+                nc.vector.tensor_copy(out=bias_wide[:], in_=bias_rows[:])
+                bias_turned = turned_pool.tile([P, WIDE], F32, name="bias_turned", tag="turned")
+                nc.tensor.transpose(bias_turned[:, 0:P], bias_wide[:], identity[:])
+                nc.vector.tensor_copy(out=bias_col[:, 0:1], in_=bias_turned[:, 0:1])
             for i, (unit, bank) in enumerate(banks_due(step)):
                 multiply_bank(unit, bank, step > UNITS and i % 2 == 1)

@@ -40,6 +40,7 @@ PIECE_COLS = P * SHIFTS // STORE_PIECES
 FLOPS = 2 * BATCH * OUT_H * OUT_W * (CHANNELS * KS * KS) * C_OUT
 
 
+FIRST_QUADS = ((0, 0), (0, 1), (0, 2))
 EARLY_UNITS = 2
 
 
@@ -152,7 +153,7 @@ def tile_conv2d_kernel(tc, x, weights_words, weights_scales, bias, out):
                 width = n_jb * 2 * P
                 src = turneds[(g, t, bank)][:, 0:width].rearrange("p (k u n) -> p k n u", k=n_jb, u=2)
                 dst = words[:, bank * WIDE : bank * WIDE + width].rearrange("p (k n u) -> p k n u", k=n_jb, u=2)
-                if n_jb == 2 or t % 2 == 1:
+                if n_jb == 2 or t % 2 == 1 or (g, t) in FIRST_QUADS:
                     nc.scalar.copy(out=dst, in_=src)
                 else:
                     nc.vector.tensor_copy(out=dst, in_=src)
@@ -265,7 +266,7 @@ def tile_conv2d_kernel(tc, x, weights_words, weights_scales, bias, out):
                 store_piece(*divmod(step - (KS - 1) - UNITS_PER_GROUP, STORE_PIECES))
             for g, t in quads_first_needed_by(step + TURN_AHEAD):
                 gather(g, t)
-            if step == 0:
+            if step == 2:
                 nc.vector.tensor_copy(out=bias_wide[:], in_=bias_rows[:])
                 bias_turned = turned_pool.tile([P, WIDE], F32, name="bias_turned", tag="turned")
                 nc.tensor.transpose(bias_turned[:, 0:P], bias_wide[:], identity[:])

@@ -18,39 +18,34 @@ OUT_W = WIDTH - KS + 1
 M_SPAN = 32
 J_BLOCKS = OUT_W // M_SPAN
 
-WINDOWS = 20
-RUNS = OUT_H // WINDOWS
-CH_GROUP = P // RUNS
-GROUPS = BATCH * CHANNELS // CH_GROUP
-ROWS_HELD = WINDOWS + KS - 1
-UNITS_PER_GROUP = WINDOWS // KS
-UNITS = GROUPS * UNITS_PER_GROUP
 WORDS = (OUT_W + 2) // 2
 PAIR_PITCH = 336
-SHIFTS = WINDOWS * J_BLOCKS
 QUAD_COLS = J_BLOCKS * P
 WIDE = 4 * P
 BANKS_PER_UNIT = KS * J_BLOCKS // 4
-FIRST_LOADS = 5
-LOADS_PER_STEP = 3
-TURN_AHEAD = 2
-STORE_PIECES = UNITS_PER_GROUP
-PIECE_COLS = P * SHIFTS // STORE_PIECES
+UNIT_COLS = KS * QUAD_COLS
+CHANNELS_PER_BLOCK = 16
+BLOCKS = BATCH * CHANNELS // CHANNELS_PER_BLOCK
+BLOCK_UNITS = 5
+UNITS = BLOCKS * BLOCK_UNITS
+SPLIT = ()
 
 FLOPS = 2 * BATCH * OUT_H * OUT_W * (CHANNELS * KS * KS) * C_OUT
 
 
-FIRST_QUADS = ((0, 0), (0, 1), (0, 2))
-EARLY_UNITS = 2
+def groups_of(block):
+    c = CHANNELS_PER_BLOCK * block
+    if block in SPLIT:
+        return [(block, 0, 2, c, 8, 16, 0), (block, 2, 2, c + 8, 8, 16, 0), (block, 4, 1, c, 16, 8, 128)]
+    return [(block, 0, 5, c, 16, 8, 0)]
 
 
-def banks_due(step):
-    due = []
-    for unit in range(UNITS):
-        for bank in range(BANKS_PER_UNIT):
-            if step == unit + ((4 * bank + 3) // J_BLOCKS if unit >= UNITS - EARLY_UNITS else KS - 1):
-                due.append((unit, bank))
-    return due
+GROUPS = [group for block in range(BLOCKS) for group in groups_of(block)]
+UNIT_LIST = [(g, t) for g in range(len(GROUPS)) for t in range(GROUPS[g][2])]
+FIRST = (0, 1, 0, 1, 2) + tuple(range(3, 18))
+SAVED = ((0, 2),)
+LAST_STEP = max(FIRST) + KS - 1
+ORDER = tuple(range(UNITS))
 
 
 def passes_of_bank(bank):
@@ -70,20 +65,13 @@ def passes_of_bank(bank):
     return passes
 
 
-def quads_first_needed_by(unit):
-    if not 0 <= unit < UNITS:
-        return []
-    g, t = divmod(unit, UNITS_PER_GROUP)
-    return [(g, 0), (g, 1)] if t == 0 else [(g, t + 1)]
-
-
 def tile_conv2d_kernel(tc, x, weights_words, weights_scales, bias, out):
     nc = tc.nc
     with ExitStack() as ctx:
         consts = ctx.enter_context(tc.tile_pool(name="consts", bufs=1))
         image_pool = ctx.enter_context(tc.tile_pool(name="image", bufs=16))
         woven_pool = ctx.enter_context(tc.tile_pool(name="woven", bufs=3))
-        quad_pool = ctx.enter_context(tc.tile_pool(name="quad", bufs=10))
+        quad_pool = ctx.enter_context(tc.tile_pool(name="quad", bufs=11))
         mx_pool = ctx.enter_context(tc.tile_pool(name="mx", bufs=14))
         result_pool = ctx.enter_context(tc.tile_pool(name="result", bufs=2))
         turned_pool = ctx.enter_context(tc.psum_pool(name="turned", bufs=4))
@@ -94,24 +82,27 @@ def tile_conv2d_kernel(tc, x, weights_words, weights_scales, bias, out):
         wovens = {}
         turneds = {}
         quads = {}
+        saved = {}
         codes = {}
         planes = {}
         results = {}
 
         def load_quad(g, t):
+            block, unit0, units, c_first, n_ch, runs, row0 = GROUPS[g]
             image = image_pool.tile([P, KS // 2, PAIR_PITCH], BF16, name="image", tag="image")
             images[(g, t)] = image
-            b, c0 = divmod(g * CH_GROUP, CHANNELS)
-            skip = KS - 1 if t == UNITS_PER_GROUP else 0
-            runs = x[b, c0 : c0 + CH_GROUP, skip : skip + OUT_H, :].rearrange("c (r k) w -> c r (k w)", k=WINDOWS)
-            if t == UNITS_PER_GROUP:
+            b, c0 = divmod(c_first, CHANNELS)
+            windows = KS * units
+            skip = KS - 1 if t == units else 0
+            rows = x[b, c0 : c0 + n_ch, row0 + skip : row0 + skip + runs * windows, :].rearrange("c (r k) w -> c r (k w)", k=windows)
+            if t == units:
                 nc.vector.memset(image[:, 1, WIDTH - 1 : 2 * WIDTH], 0.0)
             for a in range(KS // 2):
                 row = KS * t + 2 * a
-                n_rows = min(2, ROWS_HELD - row)
+                n_rows = min(2, windows + KS - 1 - row)
                 nc.sync.dma_start(
                     out=image[:, a, 0 : n_rows * WIDTH],
-                    in_=runs[:, :, (row - skip) * WIDTH : (row - skip + n_rows) * WIDTH],
+                    in_=rows[:, :, (row - skip) * WIDTH : (row - skip + n_rows) * WIDTH],
                 )
 
         def weave(g, t):
@@ -153,13 +144,13 @@ def tile_conv2d_kernel(tc, x, weights_words, weights_scales, bias, out):
                 width = n_jb * 2 * P
                 src = turneds[(g, t, bank)][:, 0:width].rearrange("p (k u n) -> p k n u", k=n_jb, u=2)
                 dst = words[:, bank * WIDE : bank * WIDE + width].rearrange("p (k n u) -> p k n u", k=n_jb, u=2)
-                if n_jb == 2 or t % 2 == 1 or (g, t) in FIRST_QUADS:
+                if n_jb == 2 or not (t in (2, 4) and g > 1):
                     nc.scalar.copy(out=dst, in_=src)
                 else:
                     nc.vector.tensor_copy(out=dst, in_=src)
 
         def quantise(unit, phase):
-            g, t = divmod(unit, UNITS_PER_GROUP)
+            g, t = UNIT_LIST[unit]
             code = mx_pool.tile([P, QUAD_COLS], U32, name="code", tag="code", align_bytes=64)
             plane = mx_pool.tile([P, QUAD_COLS], U8, name="plane", tag="plane", align_bytes=64)
             codes[(unit, phase)] = code
@@ -171,14 +162,21 @@ def tile_conv2d_kernel(tc, x, weights_words, weights_scales, bias, out):
                     in_=quads[(g, t)][:, KS * lo : KS * hi],
                 )
 
+        def save(g, t):
+            copy = quad_pool.tile([P, KS * QUAD_COLS], BF16, name="copy", tag="quad", align_bytes=64)
+            saved[(g, t)] = copy
+            nc.sync.dma_start(out=copy[:], in_=quads[(g, t)][:])
+
         def rotate(unit, phase):
-            g, t = divmod(unit, UNITS_PER_GROUP)
-            nc.sync.dma_start(out=quads[(g, t)][phase:P:KS, :], in_=quads[(g, t + 1)][phase:P:KS, :])
+            g, t = UNIT_LIST[unit]
+            source = saved.get((g, t + 1), quads[(g, t + 1)])
+            nc.sync.dma_start(out=quads[(g, t)][phase:P:KS, :], in_=source[phase:P:KS, :])
 
         def multiply_bank(unit, bank, by_vector):
-            g, t = divmod(unit, UNITS_PER_GROUP)
-            if t == 0 and bank == 0:
-                results[g] = result_pool.tile([P, P, SHIFTS], F32, name="result", tag="result")
+            g, t = UNIT_LIST[unit]
+            block, unit0, units = GROUPS[g][:3]
+            if block not in results:
+                results[block] = result_pool.tile([P, BLOCK_UNITS * UNIT_COLS], F32, name="result", tag="result")
             acc = acc_pool.tile([P, WIDE], F32, name="acc", tag="acc")
             for k, phase, jb, n in passes_of_bank(bank):
                 nc.tensor.matmul_mx(
@@ -190,10 +188,11 @@ def tile_conv2d_kernel(tc, x, weights_words, weights_scales, bias, out):
                     start=True,
                     stop=True,
                 )
+            region = results[block][:, unit0 * UNIT_COLS : (unit0 + units) * UNIT_COLS].rearrange("o (n k) -> o n k", n=P)
             first = KS * J_BLOCKS * t + 4 * bank
             if by_vector:
                 nc.vector.tensor_scalar(
-                    out=results[g][:, :, first : first + 4],
+                    out=region[:, :, first : first + 4],
                     in0=acc.rearrange("o (k n) -> o n k", k=4),
                     scalar1=bias_col[:, 0:1],
                     scalar2=None,
@@ -201,20 +200,76 @@ def tile_conv2d_kernel(tc, x, weights_words, weights_scales, bias, out):
                 )
             else:
                 nc.scalar.activation(
-                    out=results[g][:, :, first : first + 4],
+                    out=region[:, :, first : first + 4],
                     in_=acc.rearrange("o (k n) -> o n k", k=4),
                     func=mybir.ActivationFunctionType.Identity,
                     bias=bias_col[:, 0:1],
                 )
 
         def store_piece(g, piece):
-            b, c0 = divmod(g * CH_GROUP, CHANNELS)
-            rows_of_a = out[b].rearrange("o u v -> o (u v)")
-            lo = c0 * OUT_H * J_BLOCKS + piece * PIECE_COLS
-            nc.sync.dma_start(
-                out=rows_of_a[:, lo : lo + PIECE_COLS],
-                in_=results[g].rearrange("o n k -> o (n k)")[:, piece * PIECE_COLS : (piece + 1) * PIECE_COLS],
-            )
+            block, unit0, units, c_first, n_ch, runs, row0 = GROUPS[g]
+            b, c0 = divmod(c_first, CHANNELS)
+            lo = (unit0 + piece) * UNIT_COLS
+            in_ = results[block][:, lo : lo + UNIT_COLS]
+            if units == BLOCK_UNITS:
+                lo = c0 * OUT_H * J_BLOCKS + piece * UNIT_COLS
+                nc.sync.dma_start(out=out[b].rearrange("o u v -> o (u v)")[:, lo : lo + UNIT_COLS], in_=in_)
+            else:
+                n = n_ch // units
+                c0 = c0 + piece * n
+                by_channel = out[b].rearrange("o u v -> o (u v)").rearrange("o (c k) -> o c k", k=OUT_H * J_BLOCKS)
+                lo, hi = row0 * J_BLOCKS, (row0 + runs * KS * units) * J_BLOCKS
+                nc.sync.dma_start(out=by_channel[:, c0 : c0 + n, lo:hi], in_=in_.rearrange("o (c k) -> o c k", c=n))
+
+        def quads_first_needed_by(unit):
+            g, t = UNIT_LIST[unit]
+            return [(g, 0), (g, 1)] if t == 0 else [(g, t + 1)]
+
+        started = []
+
+        def prepared_in(step):
+            fresh = []
+            for u in ORDER:
+                if FIRST[u] - 1 == step:
+                    g, t = UNIT_LIST[u]
+                    for quad in ((g, t), (g, t + 1)):
+                        if quad not in started:
+                            started.append(quad)
+                            fresh.append(quad)
+            return fresh
+
+        load_order = []
+        for step in range(-4, LAST_STEP + 1):
+            load_order.extend(prepared_in(step))
+        started.clear()
+        pending = list(load_order)
+
+        def load_next(n):
+            for i in range(n):
+                if pending:
+                    load_quad(*pending.pop(0))
+
+        pieces = []
+        for g in range(len(GROUPS)):
+            done = max(FIRST[u] for u in range(UNITS) if UNIT_LIST[u][0] == g) + KS - 1
+            for piece in range(GROUPS[g][2]):
+                pieces.append((done, g, piece))
+
+        def store_next(step, n):
+            for i in range(n):
+                if pieces and pieces[0][0] < step:
+                    store_piece(*pieces.pop(0)[1:])
+
+        def early(unit):
+            return unit < 5 or unit >= UNITS - 2
+
+        def banks_due(step):
+            due = []
+            for unit in ORDER:
+                for bank in range(BANKS_PER_UNIT):
+                    if step == FIRST[unit] + ((4 * bank + 3) // J_BLOCKS if early(unit) else KS - 1):
+                        due.append((unit, bank))
+            return due
 
         identity = consts.tile([P, P], F32, name="identity")
         make_identity(nc, identity[:])
@@ -226,13 +281,7 @@ def tile_conv2d_kernel(tc, x, weights_words, weights_scales, bias, out):
         bias_col = consts.tile([P, 1], F32, name="bias_col")
         nc.vector.memset(w_plane[:].bitcast(I32), 0)
         nc.vector.memset(bias_rows[:], 0.0)
-        for g, t in quads_first_needed_by(0):
-            load_quad(g, t)
-
-        load_order = [quad for unit in range(UNITS) for quad in quads_first_needed_by(unit)]
-        for g, t in load_order[len(quads_first_needed_by(0)) : FIRST_LOADS]:
-            load_quad(g, t)
-
+        load_next(6)
         nc.sync.dma_start(out=bias_rows[0:1, :], in_=bias.rearrange("(o n) -> o n", o=1))
         w_sbuf = w_words.bitcast(I32)
         w_dram = weights_words[0].rearrange("(i q) b -> i q b", q=2 * KS).bitcast(I32)
@@ -249,27 +298,42 @@ def tile_conv2d_kernel(tc, x, weights_words, weights_scales, bias, out):
                 in_=weights_scales[0, 4 * quadrant : 4 * quadrant + 4, :].bitcast(I32),
             )
 
-        for step in range(-TURN_AHEAD, UNITS + KS - 1 + UNITS_PER_GROUP):
-            for g, t in quads_first_needed_by(step + TURN_AHEAD):
-                weave(g, t)
-                turn(g, t)
-            for phase in range(KS):
-                unit = step - phase
-                if 0 <= unit < UNITS:
-                    quantise(unit, phase)
-                    if phase < KS - 1:
-                        rotate(unit, phase)
+        for step in range(-1, LAST_STEP + 12):
+            fresh = prepared_in(step)
+            rounds = False
+            due = banks_due(step)
+            if not rounds:
+                for g, t in fresh:
+                    weave(g, t)
+                    turn(g, t)
+            for lowest in ((True, False) if rounds else (None,)):
+                for phase in range(KS):
+                    for unit in ORDER:
+                        if FIRST[unit] + phase == step and (lowest is None or (unit < BLOCK_UNITS) == lowest):
+                            quantise(unit, phase)
+                            if phase < KS - 1:
+                                rotate(unit, phase)
+                if lowest:
+                    for i, (unit, bank) in enumerate(due):
+                        if unit < BLOCK_UNITS:
+                            multiply_bank(unit, bank, False)
+                    for g, t in fresh:
+                        weave(g, t)
+                        turn(g, t)
+                        gather(g, t)
             if step >= 0:
-                for g, t in load_order[FIRST_LOADS + LOADS_PER_STEP * step : FIRST_LOADS + LOADS_PER_STEP * (step + 1)]:
-                    load_quad(g, t)
-            if 0 <= step - (KS - 1) - UNITS_PER_GROUP < UNITS:
-                store_piece(*divmod(step - (KS - 1) - UNITS_PER_GROUP, STORE_PIECES))
-            for g, t in quads_first_needed_by(step + TURN_AHEAD):
-                gather(g, t)
-            if step == 2:
+                load_next(3)
+            store_next(step, 1)
+            if not rounds:
+                for g, t in fresh:
+                    gather(g, t)
+                    if (g, t) in SAVED:
+                        save(g, t)
+            if step == 0:
                 nc.vector.tensor_copy(out=bias_wide[:], in_=bias_rows[:])
                 bias_turned = turned_pool.tile([P, WIDE], F32, name="bias_turned", tag="turned")
                 nc.tensor.transpose(bias_turned[:, 0:P], bias_wide[:], identity[:])
                 nc.vector.tensor_copy(out=bias_col[:, 0:1], in_=bias_turned[:, 0:1])
-            for i, (unit, bank) in enumerate(banks_due(step)):
-                multiply_bank(unit, bank, step > UNITS and i % 2 == 1)
+            for i, (unit, bank) in enumerate(due):
+                if not (rounds and unit < BLOCK_UNITS):
+                    multiply_bank(unit, bank, step > LAST_STEP - 2 and i % 2 == 1)

@@ -19,6 +19,7 @@ M_SPAN = 32
 J_BLOCKS = OUT_W // M_SPAN
 
 WORDS = (OUT_W + 2) // 2
+NEIGHBOURS = 3
 PAIR_PITCH = 336
 QUAD_COLS = J_BLOCKS * P
 WIDE = 4 * P
@@ -110,12 +111,14 @@ def tile_conv2d_kernel(tc, x, weights_words, weights_scales, bias, out):
             wovens[(g, t)] = woven
             image = images[(g, t)]
             nc.vector.tensor_copy(
-                out=woven.rearrange("n w s (a b) -> n w s a b", b=2)[:, :, 0, :, :],
-                in_=image.bitcast(F32)[:, :, 0 : WIDTH + 1].rearrange("n a (b w) -> n w a b", b=2)[:, 0:WORDS, :, :],
+                out=woven[:, :, 0, :].rearrange("n (c i) (a b) -> n c a b i", b=2, i=NEIGHBOURS),
+                in_=image.bitcast(F32)[:, :, 0 : WIDTH + 1]
+                .rearrange("n a (b w) -> n a b w", b=2)[:, :, :, 0:WORDS]
+                .rearrange("n a b (c i) -> n c a b i", i=NEIGHBOURS),
             )
             nc.vector.tensor_copy(
-                out=woven.bitcast(BF16).rearrange("n w s (a b e) -> n w s a b e", b=2, e=2)[:, :, 1, :, :, :],
-                in_=image[:, :, 1 : 1 + 4 * WORDS].rearrange("n a (b w e) -> n w a b e", b=2, e=2),
+                out=woven.bitcast(BF16)[:, :, 1, :].rearrange("n (c i) (a b e) -> n c a b i e", b=2, e=2, i=NEIGHBOURS),
+                in_=image[:, :, 1 : 1 + 4 * WORDS].rearrange("n a (b c i e) -> n c a b i e", b=2, e=2, i=NEIGHBOURS),
             )
 
         def jbs_of_bank(bank):

@@ -97,7 +97,7 @@ def tile_conv2d_kernel(tc, x, weights_words, weights_scales, bias, out):
             skip = KS - 1 if t == units else 0
             rows = x[b, c0 : c0 + n_ch, row0 + skip : row0 + skip + runs * windows, :].rearrange("c (r k) w -> c r (k w)", k=windows)
             if t == units:
-                nc.vector.memset(image[:, 1, WIDTH - 1 : 2 * WIDTH], 0.0)
+                nc.gpsimd.memset(image[:, 1, WIDTH - 1 : 2 * WIDTH], 0.0)
             for a in range(KS // 2):
                 row = KS * t + 2 * a
                 n_rows = min(2, windows + KS - 1 - row)
@@ -333,10 +333,10 @@ def tile_conv2d_kernel(tc, x, weights_words, weights_scales, bias, out):
                     if (g, t) in SAVED:
                         save(g, t)
             if step == 0:
-                nc.vector.tensor_copy(out=bias_wide[:], in_=bias_rows[:])
+                nc.scalar.copy(out=bias_wide[:], in_=bias_rows[:])
                 bias_turned = turned_pool.tile([P, WIDE], F32, name="bias_turned", tag="turned")
                 nc.tensor.transpose(bias_turned[:, 0:P], bias_wide[:], identity[:])
-                nc.vector.tensor_copy(out=bias_col[:, 0:1], in_=bias_turned[:, 0:1])
+                nc.scalar.copy(out=bias_col[:, 0:1], in_=bias_turned[:, 0:1])
             for i, (unit, bank) in enumerate(due):
                 if not (rounds and unit < BLOCK_UNITS):
                     multiply_bank(unit, bank, step > LAST_STEP - 2 and i % 2 == 1)

from contextlib import ExitStack

import concourse.mybir as mybir
from concourse.masks import make_identity

BF16 = mybir.dt.bfloat16
F32 = mybir.dt.float32
I32 = mybir.dt.int32
U32 = mybir.dt.uint32
U8 = mybir.dt.uint8
FP8X4 = mybir.dt.float8_e4m3fn_x4
FP4X4 = mybir.dt.float4_e2m1fn_x4

P = 128
BATCH, CHANNELS, HEIGHT, WIDTH, KS, C_OUT = 2, 32, 163, 163, 4, 128
OUT_H = HEIGHT - KS + 1
OUT_W = WIDTH - KS + 1
M_SPAN = 32
J_BLOCKS = OUT_W // M_SPAN

WORDS = (OUT_W + 2) // 2
NEIGHBOURS = 3
PAIR_PITCH = 336
QUAD_COLS = J_BLOCKS * P
WIDE = 4 * P
BANKS_PER_UNIT = KS * J_BLOCKS // 4
UNIT_COLS = KS * QUAD_COLS
CHANNELS_PER_BLOCK = 16
BLOCKS = BATCH * CHANNELS // CHANNELS_PER_BLOCK
BLOCK_UNITS = 5
UNITS = BLOCKS * BLOCK_UNITS
SPLIT = ()

FLOPS = 2 * BATCH * OUT_H * OUT_W * (CHANNELS * KS * KS) * C_OUT


def groups_of(block):
    c = CHANNELS_PER_BLOCK * block
    if block in SPLIT:
        return [(block, 0, 2, c, 8, 16, 0), (block, 2, 2, c + 8, 8, 16, 0), (block, 4, 1, c, 16, 8, 128)]
    return [(block, 0, 5, c, 16, 8, 0)]


GROUPS = [group for block in range(BLOCKS) for group in groups_of(block)]
UNIT_LIST = [(g, t) for g in range(len(GROUPS)) for t in range(GROUPS[g][2])]
FIRST = (0, 1, 0, 1, 2) + tuple(range(3, 18))
SAVED = ((0, 2),)
LAST_STEP = max(FIRST) + KS - 1
ORDER = tuple(range(UNITS))


def passes_of_bank(bank):
    runs = []
    for k in range(4):
        phase, jb = divmod(4 * bank + k, J_BLOCKS)
        if runs and runs[-1][1] == phase:
            runs[-1] = (runs[-1][0], phase, runs[-1][2], runs[-1][3] + 1)
        else:
            runs.append((k, phase, jb, 1))
    passes = []
    for k, phase, jb, n in runs:
        if n == 3:
            passes.extend([(k, phase, jb, 2), (k + 2, phase, jb + 2, 1)])
        else:
            passes.append((k, phase, jb, n))
    return passes


def tile_conv2d_kernel(tc, x, weights_words, weights_scales, bias, out):
    nc = tc.nc
    with ExitStack() as ctx:
        consts = ctx.enter_context(tc.tile_pool(name="consts", bufs=1))
        image_pool = ctx.enter_context(tc.tile_pool(name="image", bufs=16))
        woven_pool = ctx.enter_context(tc.tile_pool(name="woven", bufs=3))
        quad_pool = ctx.enter_context(tc.tile_pool(name="quad", bufs=11))
        mx_pool = ctx.enter_context(tc.tile_pool(name="mx", bufs=14))
        result_pool = ctx.enter_context(tc.tile_pool(name="result", bufs=2))
        turned_pool = ctx.enter_context(tc.psum_pool(name="turned", bufs=4))
        acc_pool = ctx.enter_context(tc.psum_pool(name="acc", bufs=4))
        ctx.enter_context(tc.manual_schedule())

        images = {}
        wovens = {}
        turneds = {}
        quads = {}
        saved = {}
        codes = {}
        planes = {}
        results = {}

        def load_quad(g, t):
            block, unit0, units, c_first, n_ch, runs, row0 = GROUPS[g]
            image = image_pool.tile([P, KS // 2, PAIR_PITCH], BF16, name="image", tag="image")
            images[(g, t)] = image
            b, c0 = divmod(c_first, CHANNELS)
            windows = KS * units
            skip = KS - 1 if t == units else 0
            rows = x[b, c0 : c0 + n_ch, row0 + skip : row0 + skip + runs * windows, :].rearrange("c (r k) w -> c r (k w)", k=windows)
            if t == units:
                nc.gpsimd.memset(image[:, 1, WIDTH - 1 : 2 * WIDTH], 0.0)
            for a in range(KS // 2):
                row = KS * t + 2 * a
                n_rows = min(2, windows + KS - 1 - row)
                nc.sync.dma_start(
                    out=image[:, a, 0 : n_rows * WIDTH],
                    in_=rows[:, :, (row - skip) * WIDTH : (row - skip + n_rows) * WIDTH],
                )

        def weave(g, t):
            woven = woven_pool.tile([P, WORDS, 2, KS], F32, name="woven", tag="woven")
            wovens[(g, t)] = woven
            image = images[(g, t)]
            nc.vector.tensor_copy(
                out=woven[:, :, 0, :].rearrange("n (c i) (a b) -> n c a b i", b=2, i=NEIGHBOURS),
                in_=image.bitcast(F32)[:, :, 0 : WIDTH + 1]
                .rearrange("n a (b w) -> n a b w", b=2)[:, :, :, 0:WORDS]
                .rearrange("n a b (c i) -> n c a b i", i=NEIGHBOURS),
            )
            nc.vector.tensor_copy(
                out=woven.bitcast(BF16)[:, :, 1, :].rearrange("n (c i) (a b e) -> n c a b i e", b=2, e=2, i=NEIGHBOURS),
                in_=image[:, :, 1 : 1 + 4 * WORDS].rearrange("n a (b c i e) -> n c a b i e", b=2, e=2, i=NEIGHBOURS),
            )

        def jbs_of_bank(bank):
            return [jb for jb in (2 * bank, 2 * bank + 1) if jb < J_BLOCKS]

        def turn(g, t):
            flat = wovens[(g, t)].rearrange("n w s h -> n (w s h)")
            for bank in range(3):
                turned = turned_pool.tile([P, WIDE], F32, name="turned", tag="turned")
                turneds[(g, t, bank)] = turned
                for k, jb in enumerate(jbs_of_bank(bank)):
                    for u in range(2):
                        first = 2 * KS * (M_SPAN // 2 * jb + u)
                        nc.tensor.transpose(
                            turned[:, (2 * k + u) * P : (2 * k + u + 1) * P],
                            flat[:, first : first + P],
                            identity[:],
                        )

        def gather(g, t):
            quad = quad_pool.tile([P, KS * QUAD_COLS], BF16, name="quad", tag="quad", align_bytes=64)
            quads[(g, t)] = quad
            words = quad.bitcast(F32)
            for bank in range(3):
                n_jb = len(jbs_of_bank(bank))
                width = n_jb * 2 * P
                src = turneds[(g, t, bank)][:, 0:width].rearrange("p (k u n) -> p k n u", k=n_jb, u=2)
                dst = words[:, bank * WIDE : bank * WIDE + width].rearrange("p (k n u) -> p k n u", k=n_jb, u=2)
                if n_jb == 2 or not (t in (2, 4) and g > 1):
                    nc.scalar.copy(out=dst, in_=src)
                else:
                    nc.vector.tensor_copy(out=dst, in_=src)

        def quantise(unit, phase):
            g, t = UNIT_LIST[unit]
            code = mx_pool.tile([P, QUAD_COLS], U32, name="code", tag="code", align_bytes=64)
            plane = mx_pool.tile([P, QUAD_COLS], U8, name="plane", tag="plane", align_bytes=64)
            codes[(unit, phase)] = code
            planes[(unit, phase)] = plane
            for lo, hi in ((0, WIDE), (WIDE, QUAD_COLS)):
                nc.vector.quantize_mx(
                    out=code[:, lo:hi].bitcast(FP8X4),
                    scales=plane[:, lo:hi],
                    in_=quads[(g, t)][:, KS * lo : KS * hi],
                )

        def save(g, t):
            copy = quad_pool.tile([P, KS * QUAD_COLS], BF16, name="copy", tag="quad", align_bytes=64)
            saved[(g, t)] = copy
            nc.sync.dma_start(out=copy[:], in_=quads[(g, t)][:])

        def rotate(unit, phase):
            g, t = UNIT_LIST[unit]
            source = saved.get((g, t + 1), quads[(g, t + 1)])
            nc.sync.dma_start(out=quads[(g, t)][phase:P:KS, :], in_=source[phase:P:KS, :])

        def multiply_bank(unit, bank, by_vector):
            g, t = UNIT_LIST[unit]
            block, unit0, units = GROUPS[g][:3]
            if block not in results:
                results[block] = result_pool.tile([P, BLOCK_UNITS * UNIT_COLS], F32, name="result", tag="result")
            acc = acc_pool.tile([P, WIDE], F32, name="acc", tag="acc")
            for k, phase, jb, n in passes_of_bank(bank):
                nc.tensor.matmul_mx(
                    out=acc[:, k * P : (k + n) * P],
                    lhsT=w_words[:, (KS - phase) % KS, :].bitcast(FP4X4),
                    lhsT_scale=w_plane[:],
                    rhs=codes[(unit, phase)][:, jb * P : (jb + n) * P].bitcast(FP8X4),
                    rhs_scale=planes[(unit, phase)][:, jb * P : (jb + n) * P],
                    start=True,
                    stop=True,
                )
            region = results[block][:, unit0 * UNIT_COLS : (unit0 + units) * UNIT_COLS].rearrange("o (n k) -> o n k", n=P)
            first = KS * J_BLOCKS * t + 4 * bank
            if by_vector:
                nc.vector.tensor_scalar(
                    out=region[:, :, first : first + 4],
                    in0=acc.rearrange("o (k n) -> o n k", k=4),
                    scalar1=bias_col[:, 0:1],
                    scalar2=None,
                    op0=mybir.AluOpType.add,
                )
            else:
                nc.scalar.activation(
                    out=region[:, :, first : first + 4],
                    in_=acc.rearrange("o (k n) -> o n k", k=4),
                    func=mybir.ActivationFunctionType.Identity,
                    bias=bias_col[:, 0:1],
                )

        def store_piece(g, piece):
            block, unit0, units, c_first, n_ch, runs, row0 = GROUPS[g]
            b, c0 = divmod(c_first, CHANNELS)
            lo = (unit0 + piece) * UNIT_COLS
            in_ = results[block][:, lo : lo + UNIT_COLS]
            if units == BLOCK_UNITS:
                lo = c0 * OUT_H * J_BLOCKS + piece * UNIT_COLS
                nc.sync.dma_start(out=out[b].rearrange("o u v -> o (u v)")[:, lo : lo + UNIT_COLS], in_=in_)
            else:
                n = n_ch // units
                c0 = c0 + piece * n
                by_channel = out[b].rearrange("o u v -> o (u v)").rearrange("o (c k) -> o c k", k=OUT_H * J_BLOCKS)
                lo, hi = row0 * J_BLOCKS, (row0 + runs * KS * units) * J_BLOCKS
                nc.sync.dma_start(out=by_channel[:, c0 : c0 + n, lo:hi], in_=in_.rearrange("o (c k) -> o c k", c=n))

        def quads_first_needed_by(unit):
            g, t = UNIT_LIST[unit]
            return [(g, 0), (g, 1)] if t == 0 else [(g, t + 1)]

        started = []

        def prepared_in(step):
            fresh = []
            for u in ORDER:
                if FIRST[u] - 1 == step:
                    g, t = UNIT_LIST[u]
                    for quad in ((g, t), (g, t + 1)):
                        if quad not in started:
                            started.append(quad)
                            fresh.append(quad)
            return fresh

        load_order = []
        for step in range(-4, LAST_STEP + 1):
            load_order.extend(prepared_in(step))
        started.clear()
        pending = list(load_order)

        def load_next(n):
            for i in range(n):
                if pending:
                    load_quad(*pending.pop(0))

        pieces = []
        for g in range(len(GROUPS)):
            done = max(FIRST[u] for u in range(UNITS) if UNIT_LIST[u][0] == g) + KS - 1
            for piece in range(GROUPS[g][2]):
                pieces.append((done, g, piece))

        def store_next(step, n):
            for i in range(n):
                if pieces and pieces[0][0] < step:
                    store_piece(*pieces.pop(0)[1:])

        def early(unit):
            return unit < 5 or unit >= UNITS - 2

        def banks_due(step):
            due = []
            for unit in ORDER:
                for bank in range(BANKS_PER_UNIT):
                    if step == FIRST[unit] + ((4 * bank + 3) // J_BLOCKS if early(unit) else KS - 1):
                        due.append((unit, bank))
            return due

        identity = consts.tile([P, P], F32, name="identity")
        make_identity(nc, identity[:])

        w_words = consts.tile([P, KS, 2 * C_OUT], U8, name="w_words", align_bytes=64)
        w_plane = consts.tile([P, C_OUT], U8, name="w_plane", align_bytes=64)
        bias_rows = consts.tile([P, P], BF16, name="bias_rows")
        bias_wide = consts.tile([P, P], F32, name="bias_wide")
        bias_col = consts.tile([P, 1], F32, name="bias_col")
        nc.vector.memset(w_plane[:].bitcast(I32), 0)
        nc.vector.memset(bias_rows[:], 0.0)
        load_next(6)
        nc.sync.dma_start(out=bias_rows[0:1, :], in_=bias.rearrange("(o n) -> o n", o=1))
        w_sbuf = w_words.bitcast(I32)
        w_dram = weights_words[0].rearrange("(i q) b -> i q b", q=2 * KS).bitcast(I32)
        for lane in range(2):
            for h in range(KS):
                first = KS * ((lane + h) % 2)
                w_rows = w_sbuf[KS * lane + h : P : 2 * KS, :, :]
                nc.sync.dma_start(out=w_rows[:, 0 : KS - h, :], in_=w_dram[:, first + h : first + KS, :])
                if h > 0:
                    nc.sync.dma_start(out=w_rows[:, KS - h : KS, :], in_=w_dram[:, first : first + h, :])
        for quadrant in range(4):
            nc.sync.dma_start(
                out=w_plane[32 * quadrant : 32 * quadrant + 4, :].bitcast(I32),
                in_=weights_scales[0, 4 * quadrant : 4 * quadrant + 4, :].bitcast(I32),
            )

        for step in range(-1, LAST_STEP + 12):
            fresh = prepared_in(step)
            rounds = False
            due = banks_due(step)
            if not rounds:
                for g, t in fresh:
                    weave(g, t)
                    turn(g, t)
            for lowest in ((True, False) if rounds else (None,)):
                for phase in range(KS):
                    for unit in ORDER:
                        if FIRST[unit] + phase == step and (lowest is None or (unit < BLOCK_UNITS) == lowest):
                            quantise(unit, phase)
                            if phase < KS - 1:
                                rotate(unit, phase)
                if lowest:
                    for i, (unit, bank) in enumerate(due):
                        if unit < BLOCK_UNITS:
                            multiply_bank(unit, bank, False)
                    for g, t in fresh:
                        weave(g, t)
                        turn(g, t)
                        gather(g, t)
            if step >= 0:
                load_next(3)
            store_next(step, 1)
            if not rounds:
                for g, t in fresh:
                    gather(g, t)
                    if (g, t) in SAVED:
                        save(g, t)
            if step == 0:
                nc.scalar.copy(out=bias_wide[:], in_=bias_rows[:])
                bias_turned = turned_pool.tile([P, WIDE], F32, name="bias_turned", tag="turned")
                nc.tensor.transpose(bias_turned[:, 0:P], bias_wide[:], identity[:])
                nc.scalar.copy(out=bias_col[:, 0:1], in_=bias_turned[:, 0:1])
            for i, (unit, bank) in enumerate(due):
                if not (rounds and unit < BLOCK_UNITS):
                    multiply_bank(unit, bank, step > LAST_STEP - 2 and i % 2 == 1)
